import numpy as np
import ml_dtypes


def mxq(x, axis, fmt="e4m3"):
    dtype, down = {"e4m3": (ml_dtypes.float8_e4m3fn, 7), "e5m2": (ml_dtypes.float8_e5m2, 14)}[fmt]
    v = np.moveaxis(np.asarray(x, np.float32).astype(ml_dtypes.bfloat16).astype(np.float64), axis, -1)
    blocks = v.reshape(v.shape[:-1] + (-1, 32))
    amax = np.abs(blocks).max(-1, keepdims=True)
    byte = np.maximum(np.where(amax > 0, np.frexp(amax)[1] - 1 + 127, 0) - down, 1)
    scale = np.exp2(byte - 127.0)
    codes = (blocks / scale).astype(np.float32).astype(dtype).astype(np.float64)
    return np.moveaxis((codes * scale).reshape(v.shape), -1, axis)


WIDE = False


def mx_kscale(k):
    if not WIDE:
        return np.ones(k)
    levels = np.array([10, -10, 5, -5, 0])
    a = np.random.permutation(np.resize(levels, k // 512 * 4)).reshape(k // 512, 4)
    idx = np.arange(k)
    return np.exp2(a[idx // 512, idx % 128 // 32])


BF16 = ml_dtypes.bfloat16


def bf(x):
    return np.asarray(x, np.float32).astype(BF16)


def f64(x):
    return np.asarray(x).astype(np.float64)


B, T, D, H, HKV, HD, R, DFF = 2, 2048, 512, 4, 2, 128, 128, 6144
HALF = HD // 2
EPS = 1e-6
THETA = 1e6


def rms_norm(x, w):
    return x / np.sqrt(np.mean(x * x, axis=-1, keepdims=True) + EPS) * w


def rotate_half(x):
    return np.concatenate([-x[..., HALF:], x[..., :HALF]], axis=-1)


def setup_inputs():
    rn = np.random.standard_normal
    s = mx_kscale(D)
    inv_freq = 1.0 / THETA ** (np.arange(HALF) / HALF)
    freqs = np.arange(T)[:, None] * inv_freq[None, :]
    emb = np.concatenate([freqs, freqs], axis=-1)
    return {
        "hidden_states": bf(rn((B, T, D)) * np.exp(0.5 * rn((B, T, 1)))),
        "ln1_w": bf((1.0 + 0.1 * rn(D)) * s),
        "Wq": bf(rn((D, H * HD)) / np.sqrt(D) / s[:, None]),
        "Wk": bf(rn((D, HKV * HD)) / np.sqrt(D) / s[:, None]),
        "Wv": bf(rn((D, HKV * HD)) / np.sqrt(D) / s[:, None]),
        "q_norm_w": bf(1.0 + 0.1 * rn(HD)),
        "k_norm_w": bf(1.0 + 0.1 * rn(HD)),
        "cos": bf(np.cos(emb)),
        "sin": bf(np.sin(emb)),
    }


def reference(hidden_states, ln1_w, Wq, Wk, Wv, q_norm_w, k_norm_w, cos, sin):
    h = rms_norm(f64(hidden_states), f64(ln1_w))
    hq = mxq(h, 2, "e4m3")
    q = rms_norm((hq @ mxq(f64(Wq), 0, "e4m3")).reshape(B, T, H, HD), f64(q_norm_w)).transpose(0, 2, 1, 3)
    k = rms_norm((hq @ mxq(f64(Wk), 0, "e4m3")).reshape(B, T, HKV, HD), f64(k_norm_w)).transpose(0, 2, 1, 3)
    v = (hq @ mxq(f64(Wv), 0, "e4m3")).reshape(B, T, HKV, HD).transpose(0, 2, 1, 3)
    c, s_ = f64(cos)[None, None], f64(sin)[None, None]
    q = q * c + rotate_half(q) * s_
    k = k * c + rotate_half(k) * s_
    return q, k, v

@@ -1,0 +1,219 @@
+from contextlib import ExitStack
+
+import concourse.mybir as mybir
+from concourse.masks import make_identity
+
+F32 = mybir.dt.float32
+BF16 = mybir.dt.bfloat16
+U32 = mybir.dt.uint32
+U8 = mybir.dt.uint8
+FP8X4 = mybir.dt.float8_e4m3fn_x4
+ALU = mybir.AluOpType
+ACT = mybir.ActivationFunctionType
+
+P = 128
+B, T, D = 2, 2048, 512
+HD = 128
+HALF = 64
+NQ, NK, NV = 4, 2, 2
+NOUT = (NQ + NK + NV) * HD
+TPP = T // P
+GRP = 4
+EPS = 1e-6
+FLOPS = 2 * B * T * D * NOUT
+
+
+def tile_rawkvinjector_pa_t_kernel(
+    tc, hidden_states, ln1_w, Wq, Wk, Wv, q_norm_w, k_norm_w, cos, sin, out_0, out_1, out_2
+):
+    nc = tc.nc
+    n_tiles = B * TPP
+    n_pairs = n_tiles // 2
+    with ExitStack() as ctx:
+        const = ctx.enter_context(tc.tile_pool(name="const", bufs=1))
+        small = ctx.enter_context(tc.tile_pool(name="small", bufs=6))
+        junk = ctx.enter_context(tc.tile_pool(name="junk", bufs=4))
+        hpool = ctx.enter_context(tc.tile_pool(name="hpool", bufs=3))
+        codes = ctx.enter_context(tc.tile_pool(name="codes", bufs=4))
+        t2pool = ctx.enter_context(tc.tile_pool(name="t2pool", bufs=4))
+        obpool = ctx.enter_context(tc.tile_pool(name="obpool", bufs=3))
+        psum_t = ctx.enter_context(tc.psum_pool(name="psum_t", bufs=2))
+        psum_a = ctx.enter_context(tc.psum_pool(name="psum_a", bufs=3))
+        psum_b = ctx.enter_context(tc.psum_pool(name="psum_b", bufs=3))
+
+        x_view = [hidden_states[b].rearrange("(p i) k -> p i k", i=TPP) for b in range(B)]
+        x_sb = {}
+        for g in range(TPP // GRP):
+            for b in range(B):
+                x_sb[(b, g)] = const.tile([P, GRP, D], BF16, name="x_%d_%d" % (b, g))
+
+        def load_x(b, g):
+            nc.sync.dma_start(out=x_sb[(b, g)][:], in_=x_view[b][:, GRP * g : GRP * (g + 1), :])
+
+        lnw_bc = const.tile([P, D], BF16)
+        nc.scalar.dma_start(out=lnw_bc[:], in_=ln1_w.partition_broadcast(P))
+        wtab = const.tile([P, 2, 2, HD], BF16)
+        nc.gpsimd.dma_start(out=wtab[:, 0, 0, :], in_=q_norm_w.partition_broadcast(P))
+        nc.gpsimd.dma_start(out=wtab[:, 0, 1, :], in_=k_norm_w.partition_broadcast(P))
+
+        load_x(0, 0)
+        wq_raw = const.tile([P, 4, NQ * HD], BF16)
+        wk_raw = const.tile([P, 4, NK * HD], BF16)
+        wv_raw = const.tile([P, 4, NV * HD], BF16)
+        nc.sync.dma_start(out=wq_raw[:], in_=Wq.rearrange("(t p) n -> p t n", p=P))
+        nc.sync.dma_start(out=wk_raw[:], in_=Wk.rearrange("(t p) n -> p t n", p=P))
+        nc.sync.dma_start(out=wv_raw[:], in_=Wv.rearrange("(t p) n -> p t n", p=P))
+        cs_raw = const.tile([P, 2, TPP, HD], BF16)
+        nc.sync.dma_start(out=cs_raw[:, 0, :, :], in_=cos.rearrange("(p i) d -> p i d", i=TPP))
+        nc.sync.dma_start(out=cs_raw[:, 1, :, :], in_=sin.rearrange("(p i) d -> p i d", i=TPP))
+        load_x(1, 0)
+        for g in range(1, TPP // GRP):
+            for b in range(B):
+                load_x(b, g)
+
+        ident = const.tile([P, P], BF16)
+        make_identity(nc, ident[:])
+        eps = const.tile([P, 1], F32)
+        nc.vector.memset(eps[:], EPS)
+
+        nc.gpsimd.tensor_scalar(
+            out=wtab[:, 1, :, 0:HALF], in0=wtab[:, 0, :, HALF:HD],
+            scalar1=-1.0, scalar2=0.0, op0=ALU.mult, op1=ALU.add,
+        )
+        nc.gpsimd.tensor_scalar(
+            out=wtab[:, 1, :, HALF:HD], in0=wtab[:, 0, :, 0:HALF],
+            scalar1=1.0, scalar2=0.0, op0=ALU.mult, op1=ALU.add,
+        )
+        tab = const.tile([P, TPP, 2, 2, HD], F32)
+
+        def build_table(i):
+            nc.gpsimd.tensor_tensor(
+                out=tab[:, i, :, :, :],
+                in0=cs_raw[:, :, i, :].unsqueeze(2).to_broadcast([P, 2, 2, HD]),
+                in1=wtab[:],
+                op=ALU.mult,
+            )
+
+        wg = const.tile([P, NOUT, 4], BF16, align_bytes=64)
+        wc = const.tile([P, NOUT], U32, align_bytes=64)
+        ws = const.tile([P, NOUT], U8, align_bytes=64)
+        nc.vector.tensor_copy(out=wg[:, 0:512, :], in_=wq_raw[:].rearrange("p t n -> p n t"))
+        nc.scalar.copy(out=wg[:, 512:768, :], in_=wk_raw[:].rearrange("p t n -> p n t"))
+        nc.scalar.copy(out=wg[:, 768:1024, :], in_=wv_raw[:].rearrange("p t n -> p n t"))
+        for c in range(2):
+            cols = slice(512 * c, 512 * (c + 1))
+            nc.vector.quantize_mx(
+                out=wc[:, cols].bitcast(FP8X4),
+                scales=ws[:, cols],
+                in_=wg[:, cols, :].rearrange("p n t -> p (n t)"),
+            )
+
+        def where(n):
+            grp = n // GRP
+            return grp % B, grp // B, n % GRP
+
+        h_codes = {}
+
+        def front(pair):
+            ss0 = small.tile([P, 2], F32)
+            for a in range(2):
+                b, g, ii = where(2 * pair + a)
+                sq = junk.tile([P, D], BF16)
+                nc.scalar.activation(
+                    out=sq[:], in_=x_sb[(b, g)][:, ii, :], func=ACT.Square, accum_out=ss0[:, a : a + 1]
+                )
+            r0 = small.tile([P, 2], F32)
+            nc.scalar.activation(
+                out=r0[:], in_=ss0[:], func=ACT.Abs_reciprocal_sqrt, scale=1.0 / D, bias=eps[:, 0:1]
+            )
+            h = hpool.tile([P, 2, D], BF16)
+            for a in range(2):
+                b, g, ii = where(2 * pair + a)
+                nc.vector.scalar_tensor_tensor(
+                    out=h[:, a, :], in0=x_sb[(b, g)][:, ii, :], scalar=r0[:, a : a + 1], in1=lnw_bc[:],
+                    op0=ALU.mult, op1=ALU.mult,
+                )
+            tp = psum_t.tile([P, 2, 4, P], BF16)
+            for a in range(2):
+                for t in range(4):
+                    nc.tensor.transpose(out=tp[:, a, t, :], in_=h[:, a, P * t : P * (t + 1)], identity=ident[:])
+            hg = hpool.tile([P, 2, P, 4], BF16, align_bytes=64)
+            nc.scalar.copy(out=hg[:], in_=tp[:].rearrange("p a t r -> p a r t"))
+            hc = codes.tile([P, 2 * P], U32, align_bytes=64)
+            hs = codes.tile([P, 2 * P], U8, align_bytes=64)
+            nc.vector.quantize_mx(
+                out=hc[:].bitcast(FP8X4), scales=hs[:], in_=hg[:].rearrange("p a r t -> p (a r t)")
+            )
+            h_codes[pair] = (hc, hs)
+
+        obs = {}
+
+        def back(n):
+            b, g, ii = where(n)
+            i = GRP * g + ii
+            if ii == 0:
+                obs[n // GRP] = obpool.tile([P, 8, GRP, HD], F32, name="ob")
+            ob = obs[n // GRP]
+            hc, hs = h_codes[n // 2]
+            tok = slice(P * (n % 2), P * (n % 2 + 1))
+            pa = psum_a.tile([P, 512], F32)
+            pb = psum_b.tile([P, 512], F32)
+            for c, acc in enumerate((pa, pb)):
+                cols = slice(512 * c, 512 * (c + 1))
+                nc.tensor.matmul_mx(
+                    out=acc[:],
+                    lhsT=hc[:, tok].bitcast(FP8X4), lhsT_scale=hs[:, tok],
+                    rhs=wc[:, cols].bitcast(FP8X4), rhs_scale=ws[:, cols],
+                    start=True, stop=True,
+                )
+            heads = [pa[:, HD * k : HD * (k + 1)] for k in range(NQ)]
+            heads += [pb[:, HD * k : HD * (k + 1)] for k in range(NK)]
+            ss = small.tile([P, 6], F32)
+            for k, u in enumerate(heads):
+                sq1 = junk.tile([P, HD], BF16)
+                nc.scalar.activation(out=sq1[:], in_=u, func=ACT.Square, accum_out=ss[:, k : k + 1])
+            nc.scalar.copy(
+                out=ob[:, 6:8, ii, :], in_=pb[:, 256:512].rearrange("p (h d) -> p h d", h=2)
+            )
+            r = small.tile([P, 6], F32)
+            nc.scalar.activation(
+                out=r[:], in_=ss[:], func=ACT.Abs_reciprocal_sqrt, scale=1.0 / HD, bias=eps[:, 0:1]
+            )
+            t2 = t2pool.tile([P, 6, HD], F32)
+            for k, u in enumerate(heads):
+                qk = 0 if k < NQ else 1
+                rk = r[:, k : k + 1]
+                nc.vector.scalar_tensor_tensor(
+                    out=ob[:, k, ii, :], in0=u, scalar=rk, in1=tab[:, i, 0, qk, :],
+                    op0=ALU.mult, op1=ALU.mult,
+                )
+                nc.vector.scalar_tensor_tensor(
+                    out=t2[:, k, 0:HALF], in0=u[:, HALF:HD], scalar=rk, in1=tab[:, i, 1, qk, 0:HALF],
+                    op0=ALU.mult, op1=ALU.mult,
+                )
+                nc.vector.scalar_tensor_tensor(
+                    out=t2[:, k, HALF:HD], in0=u[:, 0:HALF], scalar=rk, in1=tab[:, i, 1, qk, HALF:HD],
+                    op0=ALU.mult, op1=ALU.mult,
+                )
+            nc.gpsimd.tensor_tensor(
+                out=ob[:, 0:6, ii, :], in0=ob[:, 0:6, ii, :], in1=t2[:], op=ALU.add
+            )
+            if ii == GRP - 1:
+                rows = slice(GRP * g, GRP * (g + 1))
+                for dst, h0, h1 in ((out_0, 0, 4), (out_1, 4, 6), (out_2, 6, 8)):
+                    nc.sync.dma_start(
+                        out=dst[b].rearrange("h (p i) d -> p h i d", i=TPP)[:, :, rows, :],
+                        in_=ob[:, h0:h1, :, :],
+                    )
+
+        for i in range(GRP):
+            build_table(i)
+        front(0)
+        front(1)
+        for n in range(n_tiles):
+            b, g, ii = where(n)
+            if n % 2 == 0 and n // 2 + 2 < n_pairs:
+                front(n // 2 + 2)
+            if b == 0 and g + 1 < TPP // GRP:
+                build_table(GRP * (g + 1) + ii)
+            back(n)

@@ -21,6 +21,7 @@ TPP = T // P
 GRP = 4
 EPS = 1e-6
 FLOPS = 2 * B * T * D * NOUT
+REVERSED = True
 
 
 def tile_rawkvinjector_pa_t_kernel(
@@ -31,60 +32,72 @@ def tile_rawkvinjector_pa_t_kernel(
     n_pairs = n_tiles // 2
     with ExitStack() as ctx:
         const = ctx.enter_context(tc.tile_pool(name="const", bufs=1))
-        small = ctx.enter_context(tc.tile_pool(name="small", bufs=6))
+        small = ctx.enter_context(tc.tile_pool(name="small", bufs=4))
         junk = ctx.enter_context(tc.tile_pool(name="junk", bufs=4))
         hpool = ctx.enter_context(tc.tile_pool(name="hpool", bufs=3))
         codes = ctx.enter_context(tc.tile_pool(name="codes", bufs=4))
         t2pool = ctx.enter_context(tc.tile_pool(name="t2pool", bufs=4))
         obpool = ctx.enter_context(tc.tile_pool(name="obpool", bufs=3))
-        psum_t = ctx.enter_context(tc.psum_pool(name="psum_t", bufs=2))
+        psum_c = ctx.enter_context(tc.psum_pool(name="psum_c", bufs=1))
+        psum_t = ctx.enter_context(tc.psum_pool(name="psum_t", bufs=1))
         psum_a = ctx.enter_context(tc.psum_pool(name="psum_a", bufs=3))
         psum_b = ctx.enter_context(tc.psum_pool(name="psum_b", bufs=3))
+        ctx.enter_context(tc.manual_schedule())
 
+        def where(n):
+            grp = n // GRP
+            return grp % B, grp // B, n % GRP
+
+        eps = const.tile([P, 1], F32)
+        nc.vector.memset(eps[:], EPS)
+        warm = const.tile([P, 1], F32)
+        nc.scalar.activation(out=warm[:], in_=eps[:], func=ACT.Abs_reciprocal_sqrt)
+        zrow = const.tile([P, D + 2 * HD], BF16)
+        nc.vector.memset(zrow[:], 0.0)
+        ones = const.tile([P, P], BF16)
+        nc.vector.memset(ones[:], 1.0)
+        ident = const.tile([P, P], BF16)
+        make_identity(nc, ident[:])
+
+        nc.scalar.dma_start(out=zrow[0:1, 0:D], in_=ln1_w.unsqueeze(0))
+        nc.scalar.dma_start(out=zrow[0:1, D : D + HD], in_=q_norm_w.unsqueeze(0))
+        nc.scalar.dma_start(out=zrow[0:1, D + HD : D + 2 * HD], in_=k_norm_w.unsqueeze(0))
         x_view = [hidden_states[b].rearrange("(p i) k -> p i k", i=TPP) for b in range(B)]
-        x_sb = {}
-        for g in range(TPP // GRP):
-            for b in range(B):
-                x_sb[(b, g)] = const.tile([P, GRP, D], BF16, name="x_%d_%d" % (b, g))
+        x_sb = [const.tile([P, 2, D], BF16, name="x_%d" % pr) for pr in range(n_pairs)]
 
-        def load_x(b, g):
-            nc.sync.dma_start(out=x_sb[(b, g)][:], in_=x_view[b][:, GRP * g : GRP * (g + 1), :])
+        def load_x(pr):
+            b, g, ii = where(2 * pr)
+            i = GRP * g + ii
+            nc.sync.dma_start(out=x_sb[pr][:], in_=x_view[b][:, i : i + 2, :])
 
-        lnw_bc = const.tile([P, D], BF16)
-        nc.scalar.dma_start(out=lnw_bc[:], in_=ln1_w.partition_broadcast(P))
-        wtab = const.tile([P, 2, 2, HD], BF16)
-        nc.gpsimd.dma_start(out=wtab[:, 0, 0, :], in_=q_norm_w.partition_broadcast(P))
-        nc.gpsimd.dma_start(out=wtab[:, 0, 1, :], in_=k_norm_w.partition_broadcast(P))
-
-        load_x(0, 0)
+        load_x(0)
         wq_raw = const.tile([P, 4, NQ * HD], BF16)
         wk_raw = const.tile([P, 4, NK * HD], BF16)
         wv_raw = const.tile([P, 4, NV * HD], BF16)
         nc.sync.dma_start(out=wq_raw[:], in_=Wq.rearrange("(t p) n -> p t n", p=P))
         nc.sync.dma_start(out=wk_raw[:], in_=Wk.rearrange("(t p) n -> p t n", p=P))
         nc.sync.dma_start(out=wv_raw[:], in_=Wv.rearrange("(t p) n -> p t n", p=P))
+        load_x(1)
         cs_raw = const.tile([P, 2, TPP, HD], BF16)
         nc.sync.dma_start(out=cs_raw[:, 0, :, :], in_=cos.rearrange("(p i) d -> p i d", i=TPP))
         nc.sync.dma_start(out=cs_raw[:, 1, :, :], in_=sin.rearrange("(p i) d -> p i d", i=TPP))
-        load_x(1, 0)
-        for g in range(1, TPP // GRP):
-            for b in range(B):
-                load_x(b, g)
+        for pr in range(2, n_pairs):
+            load_x(pr)
 
-        ident = const.tile([P, P], BF16)
-        make_identity(nc, ident[:])
-        eps = const.tile([P, 1], F32)
-        nc.vector.memset(eps[:], EPS)
-
-        nc.gpsimd.tensor_scalar(
-            out=wtab[:, 1, :, 0:HALF], in0=wtab[:, 0, :, HALF:HD],
-            scalar1=-1.0, scalar2=0.0, op0=ALU.mult, op1=ALU.add,
+        lnw_ps = psum_c.tile([P, D], F32)
+        nc.tensor.matmul(out=lnw_ps[:], lhsT=ones[:], rhs=zrow[:, 0:D], start=True, stop=True)
+        wn_ps = psum_t.tile([P, 2, HD], F32, tag="tp")
+        nc.tensor.matmul(
+            out=wn_ps[:].rearrange("p a d -> p (a d)"), lhsT=ones[:], rhs=zrow[:, D : D + 2 * HD],
+            start=True, stop=True,
         )
-        nc.gpsimd.tensor_scalar(
-            out=wtab[:, 1, :, HALF:HD], in0=wtab[:, 0, :, 0:HALF],
-            scalar1=1.0, scalar2=0.0, op0=ALU.mult, op1=ALU.add,
-        )
+        wtab = const.tile([P, 2, 2, HD], BF16)
         tab = const.tile([P, TPP, 2, 2, HD], F32)
+
+        def norm_weight_table():
+            nc.scalar.copy(out=wtab[:, 0, :, :], in_=wn_ps[:])
+            nc.scalar.mul(out=wtab[:, 1, :, 0:HALF], in_=wn_ps[:, :, HALF:HD], mul=-1.0)
+            nc.scalar.copy(out=wtab[:, 1, :, HALF:HD], in_=wn_ps[:, :, 0:HALF])
 
         def build_table(i):
             nc.gpsimd.tensor_tensor(
@@ -97,63 +110,68 @@ def tile_rawkvinjector_pa_t_kernel(
         wg = const.tile([P, NOUT, 4], BF16, align_bytes=64)
         wc = const.tile([P, NOUT], U32, align_bytes=64)
         ws = const.tile([P, NOUT], U8, align_bytes=64)
-        nc.vector.tensor_copy(out=wg[:, 0:512, :], in_=wq_raw[:].rearrange("p t n -> p n t"))
-        nc.scalar.copy(out=wg[:, 512:768, :], in_=wk_raw[:].rearrange("p t n -> p n t"))
-        nc.scalar.copy(out=wg[:, 768:1024, :], in_=wv_raw[:].rearrange("p t n -> p n t"))
-        for c in range(2):
-            cols = slice(512 * c, 512 * (c + 1))
-            nc.vector.quantize_mx(
-                out=wc[:, cols].bitcast(FP8X4),
-                scales=ws[:, cols],
-                in_=wg[:, cols, :].rearrange("p n t -> p (n t)"),
-            )
 
-        def where(n):
-            grp = n // GRP
-            return grp % B, grp // B, n % GRP
+        def weights():
+            for raw, c0, c1 in ((wq_raw, 0, 512), (wk_raw, 512, 768), (wv_raw, 768, 1024)):
+                nc.vector.tensor_copy(
+                    out=wg[:, c0:c1, :].rearrange("p (c i) t -> p c t i", i=4),
+                    in_=raw[:].rearrange("p t (c i) -> p c t i", i=4),
+                )
+            for c in range(2):
+                cols = slice(512 * c, 512 * (c + 1))
+                nc.vector.quantize_mx(
+                    out=wc[:, cols].bitcast(FP8X4),
+                    scales=ws[:, cols],
+                    in_=wg[:, cols, :].rearrange("p n t -> p (n t)"),
+                )
 
-        h_codes = {}
+        r0s, hs_, tps, hgs, h_codes, accs, rs, obs = {}, {}, {}, {}, {}, {}, {}, {}
 
-        def front(pair):
+        def stats(pr):
             ss0 = small.tile([P, 2], F32)
             for a in range(2):
-                b, g, ii = where(2 * pair + a)
                 sq = junk.tile([P, D], BF16)
                 nc.scalar.activation(
-                    out=sq[:], in_=x_sb[(b, g)][:, ii, :], func=ACT.Square, accum_out=ss0[:, a : a + 1]
+                    out=sq[:], in_=x_sb[pr][:, a, :], func=ACT.Square, accum_out=ss0[:, a : a + 1]
                 )
             r0 = small.tile([P, 2], F32)
             nc.scalar.activation(
                 out=r0[:], in_=ss0[:], func=ACT.Abs_reciprocal_sqrt, scale=1.0 / D, bias=eps[:, 0:1]
             )
+            r0s[pr] = r0
+
+        def norm(pr):
             h = hpool.tile([P, 2, D], BF16)
             for a in range(2):
-                b, g, ii = where(2 * pair + a)
                 nc.vector.scalar_tensor_tensor(
-                    out=h[:, a, :], in0=x_sb[(b, g)][:, ii, :], scalar=r0[:, a : a + 1], in1=lnw_bc[:],
+                    out=h[:, a, :], in0=x_sb[pr][:, a, :], scalar=r0s[pr][:, a : a + 1], in1=lnw_ps[:],
                     op0=ALU.mult, op1=ALU.mult,
                 )
-            tp = psum_t.tile([P, 2, 4, P], BF16)
+            hs_[pr] = h
+
+        def transp(pr):
+            tp = psum_t.tile([P, 2, 4, P], BF16, tag="tp")
             for a in range(2):
                 for t in range(4):
-                    nc.tensor.transpose(out=tp[:, a, t, :], in_=h[:, a, P * t : P * (t + 1)], identity=ident[:])
+                    nc.tensor.transpose(
+                        out=tp[:, a, t, :], in_=hs_[pr][:, a, P * t : P * (t + 1)], identity=ident[:]
+                    )
+            tps[pr] = tp
+
+        def evac(pr):
             hg = hpool.tile([P, 2, P, 4], BF16, align_bytes=64)
-            nc.scalar.copy(out=hg[:], in_=tp[:].rearrange("p a t r -> p a r t"))
+            nc.scalar.copy(out=hg[:], in_=tps[pr][:].rearrange("p a t r -> p a r t"))
+            hgs[pr] = hg
+
+        def quant(pr):
             hc = codes.tile([P, 2 * P], U32, align_bytes=64)
             hs = codes.tile([P, 2 * P], U8, align_bytes=64)
             nc.vector.quantize_mx(
-                out=hc[:].bitcast(FP8X4), scales=hs[:], in_=hg[:].rearrange("p a r t -> p (a r t)")
+                out=hc[:].bitcast(FP8X4), scales=hs[:], in_=hgs[pr][:].rearrange("p a r t -> p (a r t)")
             )
-            h_codes[pair] = (hc, hs)
+            h_codes[pr] = (hc, hs)
 
-        obs = {}
-
-        def back(n):
-            b, g, ii = where(n)
-            i = GRP * g + ii
-            if ii == 0:
-                obs[n // GRP] = obpool.tile([P, 8, GRP, HD], F32, name="ob")
-            ob = obs[n // GRP]
+        def mx(n):
             hc, hs = h_codes[n // 2]
             tok = slice(P * (n % 2), P * (n % 2 + 1))
             pa = psum_a.tile([P, 512], F32)
@@ -168,6 +186,14 @@ def tile_rawkvinjector_pa_t_kernel(
                 )
             heads = [pa[:, HD * k : HD * (k + 1)] for k in range(NQ)]
             heads += [pb[:, HD * k : HD * (k + 1)] for k in range(NK)]
+            accs[n] = (heads, pb)
+
+        def sq_heads(n):
+            b, g, ii = where(n)
+            if ii == 0:
+                obs[n // GRP] = obpool.tile([P, 8, GRP, HD], F32, name="ob")
+            ob = obs[n // GRP]
+            heads, pb = accs[n]
             ss = small.tile([P, 6], F32)
             for k, u in enumerate(heads):
                 sq1 = junk.tile([P, HD], BF16)
@@ -179,41 +205,73 @@ def tile_rawkvinjector_pa_t_kernel(
             nc.scalar.activation(
                 out=r[:], in_=ss[:], func=ACT.Abs_reciprocal_sqrt, scale=1.0 / HD, bias=eps[:, 0:1]
             )
+            rs[n] = r
+
+        def store(grp, i0, i1):
+            b, g = grp % B, grp // B
+            rows = slice(GRP * g + i0, GRP * g + i1)
+            for dst, h0, h1 in ((out_0, 0, 4), (out_1, 4, 6), (out_2, 6, 8)):
+                nc.sync.dma_start(
+                    out=dst[b].rearrange("h (p i) d -> p h i d", i=TPP)[:, :, rows, :],
+                    in_=obs[grp][:, h0:h1, i0:i1, :],
+                )
+
+        def rope(n):
+            b, g, ii = where(n)
+            i = GRP * g + ii
+            ob = obs[n // GRP]
+            heads, pb = accs[n]
+            r = rs[n]
             t2 = t2pool.tile([P, 6, HD], F32)
             for k, u in enumerate(heads):
                 qk = 0 if k < NQ else 1
                 rk = r[:, k : k + 1]
                 nc.vector.scalar_tensor_tensor(
-                    out=ob[:, k, ii, :], in0=u, scalar=rk, in1=tab[:, i, 0, qk, :],
+                    out=ob[:, k, ii, :], in0=tab[:, i, 0, qk, :], scalar=rk, in1=u,
                     op0=ALU.mult, op1=ALU.mult,
                 )
-                nc.vector.scalar_tensor_tensor(
-                    out=t2[:, k, 0:HALF], in0=u[:, HALF:HD], scalar=rk, in1=tab[:, i, 1, qk, 0:HALF],
-                    op0=ALU.mult, op1=ALU.mult,
-                )
-                nc.vector.scalar_tensor_tensor(
-                    out=t2[:, k, HALF:HD], in0=u[:, 0:HALF], scalar=rk, in1=tab[:, i, 1, qk, HALF:HD],
-                    op0=ALU.mult, op1=ALU.mult,
-                )
-            nc.gpsimd.tensor_tensor(
-                out=ob[:, 0:6, ii, :], in0=ob[:, 0:6, ii, :], in1=t2[:], op=ALU.add
-            )
-            if ii == GRP - 1:
-                rows = slice(GRP * g, GRP * (g + 1))
-                for dst, h0, h1 in ((out_0, 0, 4), (out_1, 4, 6), (out_2, 6, 8)):
-                    nc.sync.dma_start(
-                        out=dst[b].rearrange("h (p i) d -> p h i d", i=TPP)[:, :, rows, :],
-                        in_=ob[:, h0:h1, :, :],
+                if REVERSED:
+                    nc.vector.scalar_tensor_tensor(
+                        out=t2[:, k, :].rearrange("p (s d) -> p s d", s=2),
+                        in0=tab[:, i, 1, qk, :].rearrange("p (s d) -> p s d", s=2),
+                        scalar=rk,
+                        in1=u.rearrange("p (s d) -> p s d", s=2)[:, ::-1, :],
+                        op0=ALU.mult, op1=ALU.mult,
                     )
+                else:
+                    nc.vector.scalar_tensor_tensor(
+                        out=t2[:, k, 0:HALF], in0=tab[:, i, 1, qk, 0:HALF], scalar=rk, in1=u[:, HALF:HD],
+                        op0=ALU.mult, op1=ALU.mult,
+                    )
+                    nc.vector.scalar_tensor_tensor(
+                        out=t2[:, k, HALF:HD], in0=tab[:, i, 1, qk, HALF:HD], scalar=rk, in1=u[:, 0:HALF],
+                        op0=ALU.mult, op1=ALU.mult,
+                    )
+            adder = nc.vector if n == n_tiles - 1 else nc.gpsimd
+            adder.tensor_tensor(out=ob[:, 0:6, ii, :], in0=ob[:, 0:6, ii, :], in1=t2[:], op=ALU.add)
+            if n // GRP == n_tiles // GRP - 1:
+                store(n // GRP, ii, ii + 1)
+            elif ii == GRP - 1:
+                store(n // GRP, 0, GRP)
 
-        for i in range(GRP):
-            build_table(i)
-        front(0)
-        front(1)
-        for n in range(n_tiles):
-            b, g, ii = where(n)
-            if n % 2 == 0 and n // 2 + 2 < n_pairs:
-                front(n // 2 + 2)
-            if b == 0 and g + 1 < TPP // GRP:
-                build_table(GRP * (g + 1) + ii)
-            back(n)
+        def when(f, idx, limit):
+            if 0 <= idx < limit:
+                f(idx)
+
+        for j in range(-5, n_pairs):
+            if j == -3:
+                weights()
+            when(mx, 2 * j + 2, n_tiles)
+            when(sq_heads, 2 * j + 1, n_tiles)
+            when(rope, 2 * j, n_tiles)
+            when(mx, 2 * j + 3, n_tiles)
+            when(evac, j + 3, n_pairs)
+            when(norm, j + 4, n_pairs)
+            when(transp, j + 4, n_pairs)
+            when(sq_heads, 2 * j + 2, n_tiles)
+            when(build_table, j + 4, TPP)
+            when(rope, 2 * j + 1, n_tiles)
+            when(quant, j + 2, n_pairs)
+            when(stats, j + 5, n_pairs)
+            if j == -5:
+                norm_weight_table()

@@ -22,6 +22,7 @@ GRP = 4
 EPS = 1e-6
 FLOPS = 2 * B * T * D * NOUT
 REVERSED = True
+EVAC_ON_VECTOR = (0, 1, 2, 5, 8, 11)
 
 
 def tile_rawkvinjector_pa_t_kernel(
@@ -160,7 +161,10 @@ def tile_rawkvinjector_pa_t_kernel(
 
         def evac(pr):
             hg = hpool.tile([P, 2, P, 4], BF16, align_bytes=64)
-            nc.scalar.copy(out=hg[:], in_=tps[pr][:].rearrange("p a t r -> p a r t"))
+            if pr in EVAC_ON_VECTOR:
+                nc.vector.tensor_copy(out=hg[:], in_=tps[pr][:].rearrange("p a t r -> p a r t"))
+            else:
+                nc.scalar.copy(out=hg[:], in_=tps[pr][:].rearrange("p a t r -> p a r t"))
             hgs[pr] = hg
 
         def quant(pr):
@@ -258,20 +262,20 @@ def tile_rawkvinjector_pa_t_kernel(
             if 0 <= idx < limit:
                 f(idx)
 
-        for j in range(-5, n_pairs):
-            if j == -3:
+        for j in range(-4, n_pairs):
+            if j == -2:
                 weights()
             when(mx, 2 * j + 2, n_tiles)
             when(sq_heads, 2 * j + 1, n_tiles)
             when(rope, 2 * j, n_tiles)
             when(mx, 2 * j + 3, n_tiles)
-            when(evac, j + 3, n_pairs)
-            when(norm, j + 4, n_pairs)
-            when(transp, j + 4, n_pairs)
+            when(evac, j + 2, n_pairs)
+            when(norm, j + 3, n_pairs)
+            when(transp, j + 3, n_pairs)
             when(sq_heads, 2 * j + 2, n_tiles)
-            when(build_table, j + 4, TPP)
+            when(build_table, j + 3, TPP)
             when(rope, 2 * j + 1, n_tiles)
             when(quant, j + 2, n_pairs)
-            when(stats, j + 5, n_pairs)
-            if j == -5:
+            when(stats, j + 4, n_pairs)
+            if j == -4:
                 norm_weight_table()

@@ -22,7 +22,6 @@ GRP = 4
 EPS = 1e-6
 FLOPS = 2 * B * T * D * NOUT
 REVERSED = True
-EVAC_ON_VECTOR = (0, 1, 2, 5, 8, 11)
 
 
 def tile_rawkvinjector_pa_t_kernel(
@@ -126,7 +125,7 @@ def tile_rawkvinjector_pa_t_kernel(
                     in_=wg[:, cols, :].rearrange("p n t -> p (n t)"),
                 )
 
-        r0s, hs_, tps, hgs, h_codes, accs, rs, obs = {}, {}, {}, {}, {}, {}, {}, {}
+        ss0s, r0s, hs_, tps, hgs, h_codes, accs, rs, obs = {}, {}, {}, {}, {}, {}, {}, {}, {}
 
         def stats(pr):
             ss0 = small.tile([P, 2], F32)
@@ -135,9 +134,12 @@ def tile_rawkvinjector_pa_t_kernel(
                 nc.scalar.activation(
                     out=sq[:], in_=x_sb[pr][:, a, :], func=ACT.Square, accum_out=ss0[:, a : a + 1]
                 )
+            ss0s[pr] = ss0
+
+        def stats_end(pr):
             r0 = small.tile([P, 2], F32)
             nc.scalar.activation(
-                out=r0[:], in_=ss0[:], func=ACT.Abs_reciprocal_sqrt, scale=1.0 / D, bias=eps[:, 0:1]
+                out=r0[:], in_=ss0s[pr][:], func=ACT.Abs_reciprocal_sqrt, scale=1.0 / D, bias=eps[:, 0:1]
             )
             r0s[pr] = r0
 
@@ -161,10 +163,7 @@ def tile_rawkvinjector_pa_t_kernel(
 
         def evac(pr):
             hg = hpool.tile([P, 2, P, 4], BF16, align_bytes=64)
-            if pr in EVAC_ON_VECTOR:
-                nc.vector.tensor_copy(out=hg[:], in_=tps[pr][:].rearrange("p a t r -> p a r t"))
-            else:
-                nc.scalar.copy(out=hg[:], in_=tps[pr][:].rearrange("p a t r -> p a r t"))
+            nc.scalar.copy(out=hg[:], in_=tps[pr][:].rearrange("p a t r -> p a r t"))
             hgs[pr] = hg
 
         def quant(pr):
@@ -210,17 +209,19 @@ def tile_rawkvinjector_pa_t_kernel(
                 out=r[:], in_=ss[:], func=ACT.Abs_reciprocal_sqrt, scale=1.0 / HD, bias=eps[:, 0:1]
             )
             rs[n] = r
+            if n // GRP == n_tiles // GRP - 1:
+                store(n // GRP, ii, ii + 1, (2,))
 
-        def store(grp, i0, i1):
+        def store(grp, i0, i1, parts=(0, 1, 2)):
             b, g = grp % B, grp // B
             rows = slice(GRP * g + i0, GRP * g + i1)
-            for dst, h0, h1 in ((out_0, 0, 4), (out_1, 4, 6), (out_2, 6, 8)):
+            for dst, h0, h1 in [((out_0, 0, 4), (out_1, 4, 6), (out_2, 6, 8))[w] for w in parts]:
                 nc.sync.dma_start(
                     out=dst[b].rearrange("h (p i) d -> p h i d", i=TPP)[:, :, rows, :],
                     in_=obs[grp][:, h0:h1, i0:i1, :],
                 )
 
-        def rope(n):
+        def rope(n, before_last=None):
             b, g, ii = where(n)
             i = GRP * g + ii
             ob = obs[n // GRP]
@@ -230,6 +231,8 @@ def tile_rawkvinjector_pa_t_kernel(
             for k, u in enumerate(heads):
                 qk = 0 if k < NQ else 1
                 rk = r[:, k : k + 1]
+                if k == len(heads) - 1 and before_last is not None:
+                    before_last()
                 nc.vector.scalar_tensor_tensor(
                     out=ob[:, k, ii, :], in0=tab[:, i, 0, qk, :], scalar=rk, in1=u,
                     op0=ALU.mult, op1=ALU.mult,
@@ -251,10 +254,16 @@ def tile_rawkvinjector_pa_t_kernel(
                         out=t2[:, k, HALF:HD], in0=tab[:, i, 1, qk, HALF:HD], scalar=rk, in1=u[:, 0:HALF],
                         op0=ALU.mult, op1=ALU.mult,
                     )
-            adder = nc.vector if n == n_tiles - 1 else nc.gpsimd
-            adder.tensor_tensor(out=ob[:, 0:6, ii, :], in0=ob[:, 0:6, ii, :], in1=t2[:], op=ALU.add)
+            if n == n_tiles - 1:
+                for w, h0, h1 in ((0, 0, 4), (1, 4, 6)):
+                    nc.vector.tensor_tensor(
+                        out=ob[:, h0:h1, ii, :], in0=ob[:, h0:h1, ii, :], in1=t2[:, h0:h1, :], op=ALU.add
+                    )
+                    store(n // GRP, ii, ii + 1, (w,))
+                return
+            nc.gpsimd.tensor_tensor(out=ob[:, 0:6, ii, :], in0=ob[:, 0:6, ii, :], in1=t2[:], op=ALU.add)
             if n // GRP == n_tiles // GRP - 1:
-                store(n // GRP, ii, ii + 1)
+                store(n // GRP, ii, ii + 1, (0, 1))
             elif ii == GRP - 1:
                 store(n // GRP, 0, GRP)
 
@@ -267,6 +276,7 @@ def tile_rawkvinjector_pa_t_kernel(
                 weights()
             when(mx, 2 * j + 2, n_tiles)
             when(sq_heads, 2 * j + 1, n_tiles)
+            when(stats_end, j + 3, n_pairs)
             when(rope, 2 * j, n_tiles)
             when(mx, 2 * j + 3, n_tiles)
             when(evac, j + 2, n_pairs)
@@ -274,8 +284,11 @@ def tile_rawkvinjector_pa_t_kernel(
             when(transp, j + 3, n_pairs)
             when(sq_heads, 2 * j + 2, n_tiles)
             when(build_table, j + 3, TPP)
-            when(rope, 2 * j + 1, n_tiles)
-            when(quant, j + 2, n_pairs)
+            if 0 <= 2 * j + 1 < n_tiles and 0 <= j + 2 < n_pairs:
+                rope(2 * j + 1, lambda: quant(j + 2))
+            else:
+                when(rope, 2 * j + 1, n_tiles)
+                when(quant, j + 2, n_pairs)
             when(stats, j + 4, n_pairs)
             if j == -4:
                 norm_weight_table()

@@ -71,17 +71,19 @@ def tile_rawkvinjector_pa_t_kernel(
             nc.sync.dma_start(out=x_sb[pr][:], in_=x_view[b][:, i : i + 2, :])
 
         load_x(0)
+        load_x(1)
+        load_x(2)
         wq_raw = const.tile([P, 4, NQ * HD], BF16)
         wk_raw = const.tile([P, 4, NK * HD], BF16)
         wv_raw = const.tile([P, 4, NV * HD], BF16)
         nc.sync.dma_start(out=wq_raw[:], in_=Wq.rearrange("(t p) n -> p t n", p=P))
         nc.sync.dma_start(out=wk_raw[:], in_=Wk.rearrange("(t p) n -> p t n", p=P))
         nc.sync.dma_start(out=wv_raw[:], in_=Wv.rearrange("(t p) n -> p t n", p=P))
-        load_x(1)
+        load_x(3)
         cs_raw = const.tile([P, 2, TPP, HD], BF16)
         nc.sync.dma_start(out=cs_raw[:, 0, :, :], in_=cos.rearrange("(p i) d -> p i d", i=TPP))
         nc.sync.dma_start(out=cs_raw[:, 1, :, :], in_=sin.rearrange("(p i) d -> p i d", i=TPP))
-        for pr in range(2, n_pairs):
+        for pr in range(4, n_pairs):
             load_x(pr)
 
         lnw_ps = psum_c.tile([P, D], F32)
@@ -125,7 +127,7 @@ def tile_rawkvinjector_pa_t_kernel(
                     in_=wg[:, cols, :].rearrange("p n t -> p (n t)"),
                 )
 
-        ss0s, r0s, hs_, tps, hgs, h_codes, accs, rs, obs = {}, {}, {}, {}, {}, {}, {}, {}, {}
+        r0s, hs_, tps, hgs, h_codes, accs, rs, obs = {}, {}, {}, {}, {}, {}, {}, {}
 
         def stats(pr):
             ss0 = small.tile([P, 2], F32)
@@ -134,12 +136,9 @@ def tile_rawkvinjector_pa_t_kernel(
                 nc.scalar.activation(
                     out=sq[:], in_=x_sb[pr][:, a, :], func=ACT.Square, accum_out=ss0[:, a : a + 1]
                 )
-            ss0s[pr] = ss0
-
-        def stats_end(pr):
             r0 = small.tile([P, 2], F32)
             nc.scalar.activation(
-                out=r0[:], in_=ss0s[pr][:], func=ACT.Abs_reciprocal_sqrt, scale=1.0 / D, bias=eps[:, 0:1]
+                out=r0[:], in_=ss0[:], func=ACT.Abs_reciprocal_sqrt, scale=1.0 / D, bias=eps[:, 0:1]
             )
             r0s[pr] = r0
 
@@ -209,19 +208,17 @@ def tile_rawkvinjector_pa_t_kernel(
                 out=r[:], in_=ss[:], func=ACT.Abs_reciprocal_sqrt, scale=1.0 / HD, bias=eps[:, 0:1]
             )
             rs[n] = r
-            if n // GRP == n_tiles // GRP - 1:
-                store(n // GRP, ii, ii + 1, (2,))
 
-        def store(grp, i0, i1, parts=(0, 1, 2)):
+        def store(grp, i0, i1):
             b, g = grp % B, grp // B
             rows = slice(GRP * g + i0, GRP * g + i1)
-            for dst, h0, h1 in [((out_0, 0, 4), (out_1, 4, 6), (out_2, 6, 8))[w] for w in parts]:
+            for dst, h0, h1 in ((out_0, 0, 4), (out_1, 4, 6), (out_2, 6, 8)):
                 nc.sync.dma_start(
                     out=dst[b].rearrange("h (p i) d -> p h i d", i=TPP)[:, :, rows, :],
                     in_=obs[grp][:, h0:h1, i0:i1, :],
                 )
 
-        def rope(n, before_last=None):
+        def rope(n):
             b, g, ii = where(n)
             i = GRP * g + ii
             ob = obs[n // GRP]
@@ -231,8 +228,6 @@ def tile_rawkvinjector_pa_t_kernel(
             for k, u in enumerate(heads):
                 qk = 0 if k < NQ else 1
                 rk = r[:, k : k + 1]
-                if k == len(heads) - 1 and before_last is not None:
-                    before_last()
                 nc.vector.scalar_tensor_tensor(
                     out=ob[:, k, ii, :], in0=tab[:, i, 0, qk, :], scalar=rk, in1=u,
                     op0=ALU.mult, op1=ALU.mult,
@@ -254,16 +249,10 @@ def tile_rawkvinjector_pa_t_kernel(
                         out=t2[:, k, HALF:HD], in0=tab[:, i, 1, qk, HALF:HD], scalar=rk, in1=u[:, 0:HALF],
                         op0=ALU.mult, op1=ALU.mult,
                     )
-            if n == n_tiles - 1:
-                for w, h0, h1 in ((0, 0, 4), (1, 4, 6)):
-                    nc.vector.tensor_tensor(
-                        out=ob[:, h0:h1, ii, :], in0=ob[:, h0:h1, ii, :], in1=t2[:, h0:h1, :], op=ALU.add
-                    )
-                    store(n // GRP, ii, ii + 1, (w,))
-                return
-            nc.gpsimd.tensor_tensor(out=ob[:, 0:6, ii, :], in0=ob[:, 0:6, ii, :], in1=t2[:], op=ALU.add)
+            adder = nc.vector if n == n_tiles - 1 else nc.gpsimd
+            adder.tensor_tensor(out=ob[:, 0:6, ii, :], in0=ob[:, 0:6, ii, :], in1=t2[:], op=ALU.add)
             if n // GRP == n_tiles // GRP - 1:
-                store(n // GRP, ii, ii + 1, (0, 1))
+                store(n // GRP, ii, ii + 1)
             elif ii == GRP - 1:
                 store(n // GRP, 0, GRP)
 
@@ -271,24 +260,43 @@ def tile_rawkvinjector_pa_t_kernel(
             if 0 <= idx < limit:
                 f(idx)
 
-        for j in range(-4, n_pairs):
-            if j == -2:
-                weights()
+        stats(0)
+        norm_weight_table()
+        norm(0)
+        transp(0)
+        stats(1)
+        norm(1)
+        stats(2)
+        weights()
+        evac(0)
+        transp(1)
+        quant(0)
+        mx(0)
+        mx(1)
+        build_table(0)
+        stats(3)
+        evac(1)
+        stats(4)
+        sq_heads(0)
+        build_table(1)
+        norm(2)
+        transp(2)
+        quant(1)
+        build_table(2)
+        evac(2)
+        norm(3)
+        transp(3)
+        build_table(3)
+        for j in range(n_pairs):
             when(mx, 2 * j + 2, n_tiles)
             when(sq_heads, 2 * j + 1, n_tiles)
-            when(stats_end, j + 3, n_pairs)
             when(rope, 2 * j, n_tiles)
             when(mx, 2 * j + 3, n_tiles)
-            when(evac, j + 2, n_pairs)
-            when(norm, j + 3, n_pairs)
-            when(transp, j + 3, n_pairs)
+            when(evac, j + 3, n_pairs)
+            when(norm, j + 4, n_pairs)
+            when(transp, j + 4, n_pairs)
             when(sq_heads, 2 * j + 2, n_tiles)
-            when(build_table, j + 3, TPP)
-            if 0 <= 2 * j + 1 < n_tiles and 0 <= j + 2 < n_pairs:
-                rope(2 * j + 1, lambda: quant(j + 2))
-            else:
-                when(rope, 2 * j + 1, n_tiles)
-                when(quant, j + 2, n_pairs)
-            when(stats, j + 4, n_pairs)
-            if j == -4:
-                norm_weight_table()
+            when(rope, 2 * j + 1, n_tiles)
+            when(build_table, j + 4, TPP)
+            when(quant, j + 2, n_pairs)
+            when(stats, j + 5, n_pairs)

@@ -22,6 +22,7 @@ GRP = 4
 EPS = 1e-6
 FLOPS = 2 * B * T * D * NOUT
 REVERSED = True
+EVAC_ON_VECTOR = (4, 6, 8, 10, 12)
 
 
 def tile_rawkvinjector_pa_t_kernel(
@@ -162,7 +163,10 @@ def tile_rawkvinjector_pa_t_kernel(
 
         def evac(pr):
             hg = hpool.tile([P, 2, P, 4], BF16, align_bytes=64)
-            nc.scalar.copy(out=hg[:], in_=tps[pr][:].rearrange("p a t r -> p a r t"))
+            if pr in EVAC_ON_VECTOR:
+                nc.vector.tensor_copy(out=hg[:], in_=tps[pr][:].rearrange("p a t r -> p a r t"))
+            else:
+                nc.scalar.copy(out=hg[:], in_=tps[pr][:].rearrange("p a t r -> p a r t"))
             hgs[pr] = hg
 
         def quant(pr):

@@ -21,8 +21,6 @@ TPP = T // P
 GRP = 4
 EPS = 1e-6
 FLOPS = 2 * B * T * D * NOUT
-REVERSED = True
-EVAC_ON_VECTOR = (4, 6, 8, 10, 12)
 
 
 def tile_rawkvinjector_pa_t_kernel(
@@ -37,7 +35,7 @@ def tile_rawkvinjector_pa_t_kernel(
         junk = ctx.enter_context(tc.tile_pool(name="junk", bufs=4))
         hpool = ctx.enter_context(tc.tile_pool(name="hpool", bufs=3))
         codes = ctx.enter_context(tc.tile_pool(name="codes", bufs=4))
-        t2pool = ctx.enter_context(tc.tile_pool(name="t2pool", bufs=4))
+        zpool = ctx.enter_context(tc.tile_pool(name="zpool", bufs=4))
         obpool = ctx.enter_context(tc.tile_pool(name="obpool", bufs=3))
         psum_c = ctx.enter_context(tc.psum_pool(name="psum_c", bufs=1))
         psum_t = ctx.enter_context(tc.psum_pool(name="psum_t", bufs=1))
@@ -83,7 +81,9 @@ def tile_rawkvinjector_pa_t_kernel(
         load_x(3)
         cs_raw = const.tile([P, 2, TPP, HD], BF16)
         nc.sync.dma_start(out=cs_raw[:, 0, :, :], in_=cos.rearrange("(p i) d -> p i d", i=TPP))
-        nc.sync.dma_start(out=cs_raw[:, 1, :, :], in_=sin.rearrange("(p i) d -> p i d", i=TPP))
+        sin_view = sin.rearrange("(p i) d -> p i d", i=TPP)
+        nc.sync.dma_start(out=cs_raw[:, 1, :, 0:HALF], in_=sin_view[:, :, HALF:HD])
+        nc.sync.dma_start(out=cs_raw[:, 1, :, HALF:HD], in_=sin_view[:, :, 0:HALF])
         for pr in range(4, n_pairs):
             load_x(pr)
 
@@ -99,12 +99,12 @@ def tile_rawkvinjector_pa_t_kernel(
 
         def norm_weight_table():
             nc.scalar.copy(out=wtab[:, 0, :, :], in_=wn_ps[:])
-            nc.scalar.mul(out=wtab[:, 1, :, 0:HALF], in_=wn_ps[:, :, HALF:HD], mul=-1.0)
-            nc.scalar.copy(out=wtab[:, 1, :, HALF:HD], in_=wn_ps[:, :, 0:HALF])
+            nc.scalar.copy(out=wtab[:, 1, :, 0:HALF], in_=wn_ps[:, :, 0:HALF])
+            nc.scalar.mul(out=wtab[:, 1, :, HALF:HD], in_=wn_ps[:, :, HALF:HD], mul=-1.0)
 
         def build_table(i):
             nc.gpsimd.tensor_tensor(
-                out=tab[:, i, :, :, :],
+                out=tab[:, i, :, :, :].rearrange("p q c d -> p c q d"),
                 in0=cs_raw[:, :, i, :].unsqueeze(2).to_broadcast([P, 2, 2, HD]),
                 in1=wtab[:],
                 op=ALU.mult,
@@ -163,10 +163,7 @@ def tile_rawkvinjector_pa_t_kernel(
 
         def evac(pr):
             hg = hpool.tile([P, 2, P, 4], BF16, align_bytes=64)
-            if pr in EVAC_ON_VECTOR:
-                nc.vector.tensor_copy(out=hg[:], in_=tps[pr][:].rearrange("p a t r -> p a r t"))
-            else:
-                nc.scalar.copy(out=hg[:], in_=tps[pr][:].rearrange("p a t r -> p a r t"))
+            nc.scalar.copy(out=hg[:], in_=tps[pr][:].rearrange("p a t r -> p a r t"))
             hgs[pr] = hg
 
         def quant(pr):
@@ -228,33 +225,21 @@ def tile_rawkvinjector_pa_t_kernel(
             ob = obs[n // GRP]
             heads, pb = accs[n]
             r = rs[n]
-            t2 = t2pool.tile([P, 6, HD], F32)
+            z = zpool.tile([P, 6, 2, HD], F32)
             for k, u in enumerate(heads):
                 qk = 0 if k < NQ else 1
-                rk = r[:, k : k + 1]
                 nc.vector.scalar_tensor_tensor(
-                    out=ob[:, k, ii, :], in0=tab[:, i, 0, qk, :], scalar=rk, in1=u,
+                    out=z[:, k, :, :], in0=tab[:, i, qk, :, :], scalar=r[:, k : k + 1],
+                    in1=u.unsqueeze(1).to_broadcast([P, 2, HD]),
                     op0=ALU.mult, op1=ALU.mult,
                 )
-                if REVERSED:
-                    nc.vector.scalar_tensor_tensor(
-                        out=t2[:, k, :].rearrange("p (s d) -> p s d", s=2),
-                        in0=tab[:, i, 1, qk, :].rearrange("p (s d) -> p s d", s=2),
-                        scalar=rk,
-                        in1=u.rearrange("p (s d) -> p s d", s=2)[:, ::-1, :],
-                        op0=ALU.mult, op1=ALU.mult,
-                    )
-                else:
-                    nc.vector.scalar_tensor_tensor(
-                        out=t2[:, k, 0:HALF], in0=tab[:, i, 1, qk, 0:HALF], scalar=rk, in1=u[:, HALF:HD],
-                        op0=ALU.mult, op1=ALU.mult,
-                    )
-                    nc.vector.scalar_tensor_tensor(
-                        out=t2[:, k, HALF:HD], in0=tab[:, i, 1, qk, HALF:HD], scalar=rk, in1=u[:, 0:HALF],
-                        op0=ALU.mult, op1=ALU.mult,
-                    )
             adder = nc.vector if n == n_tiles - 1 else nc.gpsimd
-            adder.tensor_tensor(out=ob[:, 0:6, ii, :], in0=ob[:, 0:6, ii, :], in1=t2[:], op=ALU.add)
+            adder.tensor_tensor(
+                out=ob[:, 0:6, ii, :].rearrange("p k (s d) -> p k s d", s=2),
+                in0=z[:, :, 0, :].rearrange("p k (s d) -> p k s d", s=2),
+                in1=z[:, :, 1, :].rearrange("p k (s d) -> p k s d", s=2)[:, :, ::-1, :],
+                op=ALU.add,
+            )
             if n // GRP == n_tiles // GRP - 1:
                 store(n // GRP, ii, ii + 1)
             elif ii == GRP - 1:

@@ -29,6 +29,8 @@ def tile_rawkvinjector_pa_t_kernel(
     nc = tc.nc
     n_tiles = B * TPP
     n_pairs = n_tiles // 2
+    BATCHES = ((0,), (1,)) + tuple((pr, pr + 1) for pr in range(2, n_pairs, 2))
+    BATCH_OF = dict((pr, bt) for bt, prs in enumerate(BATCHES) for pr in prs)
     with ExitStack() as ctx:
         const = ctx.enter_context(tc.tile_pool(name="const", bufs=1))
         small = ctx.enter_context(tc.tile_pool(name="small", bufs=4))
@@ -162,21 +164,26 @@ def tile_rawkvinjector_pa_t_kernel(
             tps[pr] = tp
 
         def evac(pr):
-            hg = hpool.tile([P, 2, P, 4], BF16, align_bytes=64)
-            nc.scalar.copy(out=hg[:], in_=tps[pr][:].rearrange("p a t r -> p a r t"))
-            hgs[pr] = hg
+            bt = BATCH_OF[pr]
+            if pr == BATCHES[bt][0]:
+                hgs[bt] = hpool.tile([P, 2 * len(BATCHES[bt]), P, 4], BF16, align_bytes=64, name="hg", tag="hg")
+            a0 = 2 * (pr - BATCHES[bt][0])
+            nc.scalar.copy(out=hgs[bt][:, a0 : a0 + 2, :, :], in_=tps[pr][:].rearrange("p a t r -> p a r t"))
 
-        def quant(pr):
-            hc = codes.tile([P, 2 * P], U32, align_bytes=64)
-            hs = codes.tile([P, 2 * P], U8, align_bytes=64)
+        def quant(bt):
+            width = 2 * P * len(BATCHES[bt])
+            hc = codes.tile([P, width], U32, align_bytes=64)
+            hs = codes.tile([P, width], U8, align_bytes=64)
             nc.vector.quantize_mx(
-                out=hc[:].bitcast(FP8X4), scales=hs[:], in_=hgs[pr][:].rearrange("p a r t -> p (a r t)")
+                out=hc[:].bitcast(FP8X4), scales=hs[:], in_=hgs[bt][:].rearrange("p a r t -> p (a r t)")
             )
-            h_codes[pr] = (hc, hs)
+            h_codes[bt] = (hc, hs)
 
         def mx(n):
-            hc, hs = h_codes[n // 2]
-            tok = slice(P * (n % 2), P * (n % 2 + 1))
+            bt = BATCH_OF[n // 2]
+            hc, hs = h_codes[bt]
+            first = n - 2 * BATCHES[bt][0]
+            tok = slice(P * first, P * (first + 1))
             pa = psum_a.tile([P, 512], F32)
             pb = psum_b.tile([P, 512], F32)
             for c, acc in enumerate((pa, pb)):
@@ -287,5 +294,6 @@ def tile_rawkvinjector_pa_t_kernel(
             when(sq_heads, 2 * j + 2, n_tiles)
             when(rope, 2 * j + 1, n_tiles)
             when(build_table, j + 4, TPP)
-            when(quant, j + 2, n_pairs)
+            if j + 3 < n_pairs and j + 3 == BATCHES[BATCH_OF[j + 3]][-1]:
+                quant(BATCH_OF[j + 3])
             when(stats, j + 5, n_pairs)

from contextlib import ExitStack

import concourse.mybir as mybir
from concourse.masks import make_identity

F32 = mybir.dt.float32
BF16 = mybir.dt.bfloat16
U32 = mybir.dt.uint32
U8 = mybir.dt.uint8
FP8X4 = mybir.dt.float8_e4m3fn_x4
ALU = mybir.AluOpType
ACT = mybir.ActivationFunctionType

P = 128
B, T, D = 2, 2048, 512
HD = 128
HALF = 64
NQ, NK, NV = 4, 2, 2
NOUT = (NQ + NK + NV) * HD
TPP = T // P
GRP = 4
EPS = 1e-6
FLOPS = 2 * B * T * D * NOUT


def tile_rawkvinjector_pa_t_kernel(
    tc, hidden_states, ln1_w, Wq, Wk, Wv, q_norm_w, k_norm_w, cos, sin, out_0, out_1, out_2
):
    nc = tc.nc
    n_tiles = B * TPP
    n_pairs = n_tiles // 2
    BATCHES = ((0,), (1,)) + tuple((pr, pr + 1) for pr in range(2, n_pairs, 2))
    BATCH_OF = dict((pr, bt) for bt, prs in enumerate(BATCHES) for pr in prs)
    with ExitStack() as ctx:
        const = ctx.enter_context(tc.tile_pool(name="const", bufs=1))
        small = ctx.enter_context(tc.tile_pool(name="small", bufs=4))
        junk = ctx.enter_context(tc.tile_pool(name="junk", bufs=4))
        hpool = ctx.enter_context(tc.tile_pool(name="hpool", bufs=3))
        codes = ctx.enter_context(tc.tile_pool(name="codes", bufs=4))
        zpool = ctx.enter_context(tc.tile_pool(name="zpool", bufs=4))
        obpool = ctx.enter_context(tc.tile_pool(name="obpool", bufs=3))
        psum_c = ctx.enter_context(tc.psum_pool(name="psum_c", bufs=1))
        psum_t = ctx.enter_context(tc.psum_pool(name="psum_t", bufs=1))
        psum_a = ctx.enter_context(tc.psum_pool(name="psum_a", bufs=3))
        psum_b = ctx.enter_context(tc.psum_pool(name="psum_b", bufs=3))
        ctx.enter_context(tc.manual_schedule())

        def where(n):
            grp = n // GRP
            return grp % B, grp // B, n % GRP

        eps = const.tile([P, 1], F32)
        nc.vector.memset(eps[:], EPS)
        warm = const.tile([P, 1], F32)
        nc.scalar.activation(out=warm[:], in_=eps[:], func=ACT.Abs_reciprocal_sqrt)
        zrow = const.tile([P, D + 2 * HD], BF16)
        nc.vector.memset(zrow[:], 0.0)
        ones = const.tile([P, P], BF16)
        nc.vector.memset(ones[:], 1.0)
        ident = const.tile([P, P], BF16)
        make_identity(nc, ident[:])

        nc.scalar.dma_start(out=zrow[0:1, 0:D], in_=ln1_w.unsqueeze(0))
        nc.scalar.dma_start(out=zrow[0:1, D : D + HD], in_=q_norm_w.unsqueeze(0))
        nc.scalar.dma_start(out=zrow[0:1, D + HD : D + 2 * HD], in_=k_norm_w.unsqueeze(0))
        x_view = [hidden_states[b].rearrange("(p i) k -> p i k", i=TPP) for b in range(B)]
        x_sb = [const.tile([P, 2, D], BF16, name="x_%d" % pr) for pr in range(n_pairs)]

        def load_x(pr):
            b, g, ii = where(2 * pr)
            i = GRP * g + ii
            nc.sync.dma_start(out=x_sb[pr][:], in_=x_view[b][:, i : i + 2, :])

        load_x(0)
        load_x(1)
        load_x(2)
        wq_raw = const.tile([P, 4, NQ * HD], BF16)
        wk_raw = const.tile([P, 4, NK * HD], BF16)
        wv_raw = const.tile([P, 4, NV * HD], BF16)
        nc.sync.dma_start(out=wq_raw[:], in_=Wq.rearrange("(t p) n -> p t n", p=P))
        nc.sync.dma_start(out=wk_raw[:], in_=Wk.rearrange("(t p) n -> p t n", p=P))
        nc.sync.dma_start(out=wv_raw[:], in_=Wv.rearrange("(t p) n -> p t n", p=P))
        load_x(3)
        cs_raw = const.tile([P, 2, TPP, HD], BF16)
        nc.sync.dma_start(out=cs_raw[:, 0, :, :], in_=cos.rearrange("(p i) d -> p i d", i=TPP))
        sin_view = sin.rearrange("(p i) d -> p i d", i=TPP)
        nc.sync.dma_start(out=cs_raw[:, 1, :, 0:HALF], in_=sin_view[:, :, HALF:HD])
        nc.sync.dma_start(out=cs_raw[:, 1, :, HALF:HD], in_=sin_view[:, :, 0:HALF])
        for pr in range(4, n_pairs):
            load_x(pr)

        lnw_ps = psum_c.tile([P, D], F32)
        nc.tensor.matmul(out=lnw_ps[:], lhsT=ones[:], rhs=zrow[:, 0:D], start=True, stop=True)
        wn_ps = psum_t.tile([P, 2, HD], F32, tag="tp")
        nc.tensor.matmul(
            out=wn_ps[:].rearrange("p a d -> p (a d)"), lhsT=ones[:], rhs=zrow[:, D : D + 2 * HD],
            start=True, stop=True,
        )
        wtab = const.tile([P, 2, 2, HD], BF16)
        tab = const.tile([P, TPP, 2, 2, HD], F32)

        def norm_weight_table():
            nc.scalar.copy(out=wtab[:, 0, :, :], in_=wn_ps[:])
            nc.scalar.copy(out=wtab[:, 1, :, 0:HALF], in_=wn_ps[:, :, 0:HALF])
            nc.scalar.mul(out=wtab[:, 1, :, HALF:HD], in_=wn_ps[:, :, HALF:HD], mul=-1.0)

        def build_table(i):
            nc.gpsimd.tensor_tensor(
                out=tab[:, i, :, :, :].rearrange("p q c d -> p c q d"),
                in0=cs_raw[:, :, i, :].unsqueeze(2).to_broadcast([P, 2, 2, HD]),
                in1=wtab[:],
                op=ALU.mult,
            )

        wg = const.tile([P, NOUT, 4], BF16, align_bytes=64)
        wc = const.tile([P, NOUT], U32, align_bytes=64)
        ws = const.tile([P, NOUT], U8, align_bytes=64)

        def weights():
            for raw, c0, c1 in ((wq_raw, 0, 512), (wk_raw, 512, 768), (wv_raw, 768, 1024)):
                nc.vector.tensor_copy(
                    out=wg[:, c0:c1, :].rearrange("p (c i) t -> p c t i", i=4),
                    in_=raw[:].rearrange("p t (c i) -> p c t i", i=4),
                )
            for c in range(2):
                cols = slice(512 * c, 512 * (c + 1))
                nc.vector.quantize_mx(
                    out=wc[:, cols].bitcast(FP8X4),
                    scales=ws[:, cols],
                    in_=wg[:, cols, :].rearrange("p n t -> p (n t)"),
                )

        r0s, hs_, tps, hgs, h_codes, accs, rs, obs = {}, {}, {}, {}, {}, {}, {}, {}

        def stats(pr):
            ss0 = small.tile([P, 2], F32)
            for a in range(2):
                sq = junk.tile([P, D], BF16)
                nc.scalar.activation(
                    out=sq[:], in_=x_sb[pr][:, a, :], func=ACT.Square, accum_out=ss0[:, a : a + 1]
                )
            r0 = small.tile([P, 2], F32)
            nc.scalar.activation(
                out=r0[:], in_=ss0[:], func=ACT.Abs_reciprocal_sqrt, scale=1.0 / D, bias=eps[:, 0:1]
            )
            r0s[pr] = r0

        def norm(pr):
            h = hpool.tile([P, 2, D], BF16)
            for a in range(2):
                nc.vector.scalar_tensor_tensor(
                    out=h[:, a, :], in0=x_sb[pr][:, a, :], scalar=r0s[pr][:, a : a + 1], in1=lnw_ps[:],
                    op0=ALU.mult, op1=ALU.mult,
                )
            hs_[pr] = h

        def transp(pr):
            tp = psum_t.tile([P, 2, 4, P], BF16, tag="tp")
            for a in range(2):
                for t in range(4):
                    nc.tensor.transpose(
                        out=tp[:, a, t, :], in_=hs_[pr][:, a, P * t : P * (t + 1)], identity=ident[:]
                    )
            tps[pr] = tp

        def evac(pr):
            bt = BATCH_OF[pr]
            if pr == BATCHES[bt][0]:
                hgs[bt] = hpool.tile([P, 2 * len(BATCHES[bt]), P, 4], BF16, align_bytes=64, name="hg", tag="hg")
            a0 = 2 * (pr - BATCHES[bt][0])
            nc.scalar.copy(out=hgs[bt][:, a0 : a0 + 2, :, :], in_=tps[pr][:].rearrange("p a t r -> p a r t"))

        def quant(bt):
            width = 2 * P * len(BATCHES[bt])
            hc = codes.tile([P, width], U32, align_bytes=64)
            hs = codes.tile([P, width], U8, align_bytes=64)
            nc.vector.quantize_mx(
                out=hc[:].bitcast(FP8X4), scales=hs[:], in_=hgs[bt][:].rearrange("p a r t -> p (a r t)")
            )
            h_codes[bt] = (hc, hs)

        def mx(n):
            bt = BATCH_OF[n // 2]
            hc, hs = h_codes[bt]
            first = n - 2 * BATCHES[bt][0]
            tok = slice(P * first, P * (first + 1))
            pa = psum_a.tile([P, 512], F32)
            pb = psum_b.tile([P, 512], F32)
            for c, acc in enumerate((pa, pb)):
                cols = slice(512 * c, 512 * (c + 1))
                nc.tensor.matmul_mx(
                    out=acc[:],
                    lhsT=hc[:, tok].bitcast(FP8X4), lhsT_scale=hs[:, tok],
                    rhs=wc[:, cols].bitcast(FP8X4), rhs_scale=ws[:, cols],
                    start=True, stop=True,
                )
            heads = [pa[:, HD * k : HD * (k + 1)] for k in range(NQ)]
            heads += [pb[:, HD * k : HD * (k + 1)] for k in range(NK)]
            accs[n] = (heads, pb)

        def sq_heads(n):
            b, g, ii = where(n)
            if ii == 0:
                obs[n // GRP] = obpool.tile([P, 8, GRP, HD], F32, name="ob")
            ob = obs[n // GRP]
            heads, pb = accs[n]
            ss = small.tile([P, 6], F32)
            for k, u in enumerate(heads):
                sq1 = junk.tile([P, HD], BF16)
                nc.scalar.activation(out=sq1[:], in_=u, func=ACT.Square, accum_out=ss[:, k : k + 1])
            nc.scalar.copy(
                out=ob[:, 6:8, ii, :], in_=pb[:, 256:512].rearrange("p (h d) -> p h d", h=2)
            )
            r = small.tile([P, 6], F32)
            nc.scalar.activation(
                out=r[:], in_=ss[:], func=ACT.Abs_reciprocal_sqrt, scale=1.0 / HD, bias=eps[:, 0:1]
            )
            rs[n] = r

        def store(grp, i0, i1):
            b, g = grp % B, grp // B
            rows = slice(GRP * g + i0, GRP * g + i1)
            for dst, h0, h1 in ((out_0, 0, 4), (out_1, 4, 6), (out_2, 6, 8)):
                nc.sync.dma_start(
                    out=dst[b].rearrange("h (p i) d -> p h i d", i=TPP)[:, :, rows, :],
                    in_=obs[grp][:, h0:h1, i0:i1, :],
                )

        def rope(n):
            b, g, ii = where(n)
            i = GRP * g + ii
            ob = obs[n // GRP]
            heads, pb = accs[n]
            r = rs[n]
            z = zpool.tile([P, 6, 2, HD], F32)
            for k, u in enumerate(heads):
                qk = 0 if k < NQ else 1
                nc.vector.scalar_tensor_tensor(
                    out=z[:, k, :, :], in0=tab[:, i, qk, :, :], scalar=r[:, k : k + 1],
                    in1=u.unsqueeze(1).to_broadcast([P, 2, HD]),
                    op0=ALU.mult, op1=ALU.mult,
                )
            adder = nc.vector if n == n_tiles - 1 else nc.gpsimd
            adder.tensor_tensor(
                out=ob[:, 0:6, ii, :].rearrange("p k (s d) -> p k s d", s=2),
                in0=z[:, :, 0, :].rearrange("p k (s d) -> p k s d", s=2),
                in1=z[:, :, 1, :].rearrange("p k (s d) -> p k s d", s=2)[:, :, ::-1, :],
                op=ALU.add,
            )
            if n // GRP == n_tiles // GRP - 1:
                store(n // GRP, ii, ii + 1)
            elif ii == GRP - 1:
                store(n // GRP, 0, GRP)

        def when(f, idx, limit):
            if 0 <= idx < limit:
                f(idx)

        stats(0)
        norm_weight_table()
        norm(0)
        transp(0)
        stats(1)
        norm(1)
        stats(2)
        weights()
        evac(0)
        transp(1)
        quant(0)
        mx(0)
        mx(1)
        build_table(0)
        stats(3)
        evac(1)
        stats(4)
        sq_heads(0)
        build_table(1)
        norm(2)
        transp(2)
        quant(1)
        build_table(2)
        evac(2)
        norm(3)
        transp(3)
        build_table(3)
        for j in range(n_pairs):
            when(mx, 2 * j + 2, n_tiles)
            when(sq_heads, 2 * j + 1, n_tiles)
            when(rope, 2 * j, n_tiles)
            when(mx, 2 * j + 3, n_tiles)
            when(evac, j + 3, n_pairs)
            when(norm, j + 4, n_pairs)
            when(transp, j + 4, n_pairs)
            when(sq_heads, 2 * j + 2, n_tiles)
            when(rope, 2 * j + 1, n_tiles)
            when(build_table, j + 4, TPP)
            if j + 3 < n_pairs and j + 3 == BATCHES[BATCH_OF[j + 3]][-1]:
                quant(BATCH_OF[j + 3])
            when(stats, j + 5, n_pairs)
